import numpy as np
import ml_dtypes


def mxq(x, axis, fmt="e4m3"):
    dtype, down = {"e4m3": (ml_dtypes.float8_e4m3fn, 7), "e5m2": (ml_dtypes.float8_e5m2, 14)}[fmt]
    v = np.moveaxis(np.asarray(x, np.float32).astype(ml_dtypes.bfloat16).astype(np.float64), axis, -1)
    blocks = v.reshape(v.shape[:-1] + (-1, 32))
    amax = np.abs(blocks).max(-1, keepdims=True)
    byte = np.maximum(np.where(amax > 0, np.frexp(amax)[1] - 1 + 127, 0) - down, 1)
    scale = np.exp2(byte - 127.0)
    codes = (blocks / scale).astype(np.float32).astype(dtype).astype(np.float64)
    return np.moveaxis((codes * scale).reshape(v.shape), -1, axis)


WIDE = False


def mx_kscale(k):
    if not WIDE:
        return np.ones(k)
    levels = np.array([10, -10, 5, -5, 0])
    a = np.random.permutation(np.resize(levels, k // 512 * 4)).reshape(k // 512, 4)
    idx = np.arange(k)
    return np.exp2(a[idx // 512, idx % 128 // 32])


BF16 = ml_dtypes.bfloat16


def bf(x):
    return np.asarray(x, np.float32).astype(BF16)


def f64(x):
    return np.asarray(x).astype(np.float64)


E2M1 = np.array([0.0, 0.5, 1.0, 1.5, 2.0, 3.0, 4.0, 6.0, -0.0, -0.5, -1.0, -1.5, -2.0, -3.0, -4.0, -6.0])


def pack_weight(w, fmt):
    k, n = w.shape
    w = f64(bf(w)).reshape(k // 32, 32, n)
    amax = np.abs(w).max(1)
    if fmt == "e4m3":
        byte = np.frexp(amax)[1] - 1 + 127 - 7
    else:
        mant, ex = np.frexp(amax / 6.0)
        byte = np.where(mant > 0.5, ex, ex - 1) + 127
    byte = np.clip(np.where(amax > 0, byte, 1), 1, 254)
    scaled = (w * np.exp2(127.0 - byte)[:, None, :]).reshape(k, n).astype(np.float32)
    by_word = np.ascontiguousarray(scaled.reshape(k // 512, 128, 4, n).transpose(0, 1, 3, 2))
    if fmt == "e4m3":
        words = by_word.astype(ml_dtypes.float8_e4m3fn).view(np.uint8)
    else:
        c = by_word.astype(ml_dtypes.float4_e2m1fn).view(np.uint8) & 0xF
        words = c[..., 0::2] | (c[..., 1::2] << 4)
    return np.ascontiguousarray(words), np.ascontiguousarray(byte.astype(np.uint8).reshape(k // 512, 16, n))


def unpack_weight(words, scales, fmt):
    g, p, n, _ = words.shape
    if fmt == "e4m3":
        vals = np.ascontiguousarray(words).view(ml_dtypes.float8_e4m3fn).astype(np.float64)
    else:
        nib = np.empty((g, p, n, 4), np.uint8)
        nib[..., 0::2] = words & 0xF
        nib[..., 1::2] = words >> 4
        vals = E2M1[nib]
    vals = vals * np.repeat(np.exp2(scales.astype(np.float64) - 127.0), 8, axis=1)[..., None]
    return vals.transpose(0, 1, 3, 2).reshape(g * 512, n)


G, S, M, H, E, C = 8, 1024, 512, 512, 8, 64


def setup_inputs():
    s, t = mx_kscale(S), mx_kscale(M)
    dispatch_mask = bf(np.random.standard_normal((G, S, E, C)) * 0.1 * s[None, :, None, None])
    x = bf(np.random.standard_normal((G, S, M)) / s[None, :, None] * t)
    wi = np.random.standard_normal((E, M, H)) * 10.0 / np.sqrt(S * M) / t[None, :, None]
    wi_words, wi_scales = pack_weight(wi.reshape(-1, H), "e4m3")
    return {"dispatch_mask": dispatch_mask,
            "x": x,
            "wi_words": wi_words,
            "wi_scales": wi_scales}


def reference(dispatch_mask, x, wi_words, wi_scales):
    dm = mxq(f64(dispatch_mask).reshape(G, S, E * C), 1, "e4m3")
    xq = mxq(f64(x), 1, "e4m3")
    d = dm.transpose(0, 2, 1) @ xq
    dispatched = d.reshape(G, E, C, M).transpose(1, 0, 2, 3)
    pre = mxq(dispatched.reshape(E, G * C, M), 2, "e4m3") @ unpack_weight(wi_words, wi_scales, "e4m3").reshape(E, M, H)
    return np.maximum(pre, 0.0).reshape(E, G, C, H)

@@ -1,0 +1,186 @@
+from contextlib import ExitStack
+
+import concourse.mybir as mybir
+
+BF16 = mybir.dt.bfloat16
+F32 = mybir.dt.float32
+I32 = mybir.dt.int32
+U32 = mybir.dt.uint32
+U8 = mybir.dt.uint8
+FP8X4 = mybir.dt.float8_e4m3fn_x4
+RELU = mybir.ActivationFunctionType.Relu
+
+G, S, M, H, E, C = 8, 1024, 512, 512, 8, 64
+P = 128
+PACK = 4
+K_PASS = P * PACK
+PASSES = S // K_PASS
+SLOTS = E * C
+PAIRS = G // 2
+EXPERTS_PER_BANK = P // C
+BANKS = SLOTS // P
+HALF = E // 2
+LOOKAHEAD = 4
+
+FLOPS = 2 * G * S * SLOTS * M + 2 * E * G * C * M * H
+
+
+def tile_flaxpositionwisemoelayer_pa_t_e_kernel(tc, dispatch_mask, x, wi_words, wi_scales, out):
+    nc = tc.nc
+
+    mask_rows = dispatch_mask.rearrange("g (k p j) e c -> g k p (j e c)", k=PASSES, p=P, j=PACK)
+    x_rows = x.rearrange("g (k p j) m -> g k p (j m)", k=PASSES, p=P, j=PACK)
+
+    with ExitStack() as ctx:
+        consts = ctx.enter_context(tc.tile_pool(name="consts", bufs=1))
+        raw = ctx.enter_context(tc.tile_pool(name="raw", bufs=LOOKAHEAD + 2))
+        grouped = ctx.enter_context(tc.tile_pool(name="grouped", bufs=2))
+        codes = ctx.enter_context(tc.tile_pool(name="codes", bufs=3))
+        middle = ctx.enter_context(tc.tile_pool(name="middle", bufs=2))
+        results = ctx.enter_context(tc.tile_pool(name="results", bufs=12))
+        psum_d = ctx.enter_context(tc.psum_pool(name="psum_d", bufs=BANKS))
+        psum_h = ctx.enter_context(tc.psum_pool(name="psum_h", bufs=HALF))
+        ctx.enter_context(tc.manual_schedule())
+
+        wi_codes = consts.tile([P, E, H], U32, name="wi_codes", align_bytes=64)
+        wi_planes = consts.tile([P, E // 4, H], U8, name="wi_planes", align_bytes=64)
+
+        mask_raw, x_raw = {}, {}
+        mask_late = {}
+        mask_codes, mask_scales, x_codes, x_scales = {}, {}, {}, {}
+        d_grouped, d_codes, d_scales = {}, {}, {}
+
+        def load_group(g):
+            mask_raw[g] = raw.tile([P, PASSES, PACK * SLOTS], BF16, name="mask_raw")
+            x_raw[g] = raw.tile([P, PASSES, PACK * M], BF16, name="x_raw")
+            for k in range(PASSES):
+                nc.sync.dma_start(out=mask_raw[g][:, k, :], in_=mask_rows[g, k])
+                nc.sync.dma_start(out=x_raw[g][:, k, :], in_=x_rows[g, k])
+
+        def load_weights():
+            for a in range(E // 4):
+                for q in range(4):
+                    nc.sync.dma_start(
+                        out=wi_planes[32 * q : 32 * q + 16, a, :].bitcast(I32),
+                        in_=wi_scales[4 * a : 4 * a + 4, 4 * q : 4 * q + 4, :].bitcast(I32),
+                    )
+            for a in range(E // 4):
+                nc.sync.dma_start(
+                    out=wi_codes[:, 4 * a : 4 * a + 4, :].bitcast(I32),
+                    in_=wi_words[4 * a : 4 * a + 4].rearrange("e p n t -> p e (n t)").bitcast(I32),
+                )
+
+        def regroup_mask(copy, g, k):
+            tile = grouped.tile([P, SLOTS, PACK], BF16, name="mask_grouped%d" % k, align_bytes=64)
+            copy(
+                out=tile[:].rearrange("p (c i) j -> p c j i", i=4),
+                in_=mask_raw[g][:, k, :].rearrange("p (j c i) -> p c j i", j=PACK, i=4),
+            )
+            return tile
+
+        def regroup_x(g, k):
+            tile = grouped.tile([P, PACK, P, PACK], BF16, name="x_grouped%d" % k, align_bytes=64)
+            nc.vector.tensor_copy(
+                out=tile[:],
+                in_=x_raw[g][:, k, :].rearrange("p (j q t) -> p t q j", j=PACK, t=PACK),
+            )
+            return tile
+
+        def quantise(tile, words, plane):
+            nc.vector.quantize_mx(out=words.bitcast(FP8X4), scales=plane, in_=tile)
+
+        def scalar_regroup(g):
+            mask_late[g] = regroup_mask(nc.scalar.copy, g, 1)
+
+        def prepare(g):
+            mask_codes[g] = codes.tile([P, PASSES, SLOTS], U32, name="mask_codes", align_bytes=64)
+            mask_scales[g] = codes.tile([P, PASSES, SLOTS], U8, name="mask_scales", align_bytes=64)
+            x_codes[g] = codes.tile([P, PASSES, M], U32, name="x_codes", align_bytes=64)
+            x_scales[g] = codes.tile([P, PASSES, M], U8, name="x_scales", align_bytes=64)
+            mask0 = regroup_mask(nc.vector.tensor_copy, g, 0)
+            x0 = regroup_x(g, 0)
+            quantise(mask0[:].rearrange("p w j -> p (w j)"), mask_codes[g][:, 0, :], mask_scales[g][:, 0, :])
+            x1 = regroup_x(g, 1)
+            quantise(x0[:].rearrange("p t q j -> p (t q j)"), x_codes[g][:, 0, :], x_scales[g][:, 0, :])
+            quantise(mask_late[g][:].rearrange("p w j -> p (w j)"), mask_codes[g][:, 1, :], mask_scales[g][:, 1, :])
+            quantise(x1[:].rearrange("p t q j -> p (t q j)"), x_codes[g][:, 1, :], x_scales[g][:, 1, :])
+
+        def dispatch(g, share):
+            pair, member = divmod(g, 2)
+            if member == 0:
+                d_grouped[pair] = middle.tile([P, E, 2, C, PACK], BF16, name="d_grouped", align_bytes=64)
+            for b in range(BANKS):
+                bank = psum_d.tile([P, PACK, P], F32, name="bank")
+                slots = slice(P * b, P * (b + 1))
+                for t in range(PACK):
+                    cols = slice(P * t, P * (t + 1))
+                    for k in range(PASSES):
+                        nc.tensor.matmul_mx(
+                            out=bank[:, t, :],
+                            lhsT=x_codes[g][:, k, cols].bitcast(FP8X4),
+                            lhsT_scale=x_scales[g][:, k, cols],
+                            rhs=mask_codes[g][:, k, slots].bitcast(FP8X4),
+                            rhs_scale=mask_scales[g][:, k, slots],
+                            start=(k == 0),
+                            stop=(k == PASSES - 1),
+                        )
+                copy = nc.vector.tensor_copy if share and b % 2 == 1 else nc.scalar.copy
+                copy(
+                    out=d_grouped[pair][:, EXPERTS_PER_BANK * b : EXPERTS_PER_BANK * (b + 1), member, :, :],
+                    in_=bank[:].rearrange("p t (e c) -> p e c t", e=EXPERTS_PER_BANK),
+                )
+                if member == 1 and b % 2 == 1:
+                    quantise_dispatched(pair, b // 2)
+
+        def quantise_dispatched(pair, half):
+            if half == 0:
+                d_codes[pair] = middle.tile([P, E * P], U32, name="d_codes", align_bytes=64)
+                d_scales[pair] = middle.tile([P, E * P], U8, name="d_scales", align_bytes=64)
+            cols = slice(HALF * P * half, HALF * P * (half + 1))
+            quantise(
+                d_grouped[pair][:, HALF * half : HALF * (half + 1), :, :, :].rearrange("p e g c t -> p (e g c t)"),
+                d_codes[pair][:, cols],
+                d_scales[pair][:, cols],
+            )
+
+        def project(pair, half, share):
+            for e in range(HALF * half, HALF * (half + 1)):
+                cols = slice(P * e, P * (e + 1))
+                acc = psum_h.tile([P, H], F32, name="acc")
+                nc.tensor.matmul_mx(
+                    out=acc[:],
+                    lhsT=d_codes[pair][:, cols].bitcast(FP8X4),
+                    lhsT_scale=d_scales[pair][:, cols],
+                    rhs=wi_codes[:, e, :].bitcast(FP8X4),
+                    rhs_scale=wi_planes[4 * (e % 4) : P, e // 4, :],
+                    start=True,
+                    stop=True,
+                )
+                res = results.tile([P, H], F32, name="res")
+                if share and e % 2 == 1:
+                    nc.vector.tensor_scalar_max(out=res[:], in0=acc[:], scalar1=0.0)
+                else:
+                    nc.scalar.activation(out=res[:], in_=acc[:], func=RELU)
+                nc.sync.dma_start(
+                    out=out[e, 2 * pair : 2 * pair + 2, :, :].rearrange("g c h -> (g c) h"), in_=res[:]
+                )
+
+        nc.vector.memset(wi_planes[:].bitcast(I32), 0)
+        for g in range(LOOKAHEAD):
+            load_group(g)
+        load_weights()
+        scalar_regroup(0)
+
+        for step in range(G + 2):
+            share = step >= G
+            if step + LOOKAHEAD < G:
+                load_group(step + LOOKAHEAD)
+            if step < G:
+                prepare(step)
+            if 1 <= step <= G:
+                dispatch(step - 1, share)
+            if step + 1 < G:
+                scalar_regroup(step + 1)
+            if step >= 2:
+                pair, half = divmod(step - 2, 2)
+                project(pair, half, share)

@@ -81,8 +81,8 @@ def tile_flaxpositionwisemoelayer_pa_t_e_kernel(tc, dispatch_mask, x, wi_words, 
         def regroup_x(g, k):
             tile = grouped.tile([P, PACK, P, PACK], BF16, name="x_grouped%d" % k, align_bytes=64)
             nc.vector.tensor_copy(
-                out=tile[:],
-                in_=x_raw[g][:, k, :].rearrange("p (j q t) -> p t q j", j=PACK, t=PACK),
+                out=tile[:].rearrange("p t q j -> p q j t"),
+                in_=x_raw[g][:, k, :].rearrange("p (j q t) -> p q j t", j=PACK, t=PACK),
             )
             return tile
 

@@ -1,6 +1,7 @@
 from contextlib import ExitStack
 
 import concourse.mybir as mybir
+from concourse.masks import make_identity
 
 BF16 = mybir.dt.bfloat16
 F32 = mybir.dt.float32
@@ -20,167 +21,272 @@ PAIRS = G // 2
 EXPERTS_PER_BANK = P // C
 BANKS = SLOTS // P
 HALF = E // 2
+
 LOOKAHEAD = 4
+RAW_BUFS = 6
+Q_BY_GROUP = (0, 0, 0, 0, 0, 0, 0, 0)
+D_BANKS, H_BANKS, R_BANKS = 4, 4, 0
+PE_REGROUP = False
+W_SCALAR = 0
+HEAD_PIECES = 1
+BIG_LOADS = False
+STORE_N = 1
+RES_BUFS = 12
+LAST_BUFS = 12
+W_AFTER = (4, 4)
+SCALES_AFTER = (4, 4)
+FINE_TAIL = True
+TAIL_LAG = 2
+E_LAG = 1
+TAIL_E_VECTOR = True
+TAIL_R_SHARE = False
+LATE_SHARE_STEP = 8
+HEAD_SPLIT = 1
 
 FLOPS = 2 * G * S * SLOTS * M + 2 * E * G * C * M * H
 
 
 def tile_flaxpositionwisemoelayer_pa_t_e_kernel(tc, dispatch_mask, x, wi_words, wi_scales, out):
     nc = tc.nc
-
-    mask_rows = dispatch_mask.rearrange("g (k p j) e c -> g k p (j e c)", k=PASSES, p=P, j=PACK)
-    x_rows = x.rearrange("g (k p j) m -> g k p (j m)", k=PASSES, p=P, j=PACK)
+    mask_rows = dispatch_mask.rearrange("g (k p j) e c -> g p k j (e c)", k=PASSES, p=P, j=PACK)
+    x_rows = x.rearrange("g (k p j) m -> g p k j m", k=PASSES, p=P, j=PACK)
 
     with ExitStack() as ctx:
         consts = ctx.enter_context(tc.tile_pool(name="consts", bufs=1))
-        raw = ctx.enter_context(tc.tile_pool(name="raw", bufs=LOOKAHEAD + 2))
+        raw = ctx.enter_context(tc.tile_pool(name="raw", bufs=RAW_BUFS))
         grouped = ctx.enter_context(tc.tile_pool(name="grouped", bufs=2))
         codes = ctx.enter_context(tc.tile_pool(name="codes", bufs=3))
         middle = ctx.enter_context(tc.tile_pool(name="middle", bufs=2))
-        results = ctx.enter_context(tc.tile_pool(name="results", bufs=12))
-        psum_d = ctx.enter_context(tc.psum_pool(name="psum_d", bufs=BANKS))
-        psum_h = ctx.enter_context(tc.psum_pool(name="psum_h", bufs=HALF))
+        results = ctx.enter_context(tc.tile_pool(name="results", bufs=RES_BUFS))
+        psum_d = ctx.enter_context(tc.psum_pool(name="psum_d", bufs=D_BANKS))
+        psum_h = ctx.enter_context(tc.psum_pool(name="psum_h", bufs=H_BANKS))
+        psum_r = ctx.enter_context(tc.psum_pool(name="psum_r", bufs=max(R_BANKS, 1)))
         ctx.enter_context(tc.manual_schedule())
 
         wi_codes = consts.tile([P, E, H], U32, name="wi_codes", align_bytes=64)
         wi_planes = consts.tile([P, E // 4, H], U8, name="wi_planes", align_bytes=64)
+        ident = consts.tile([P, P], BF16, name="ident")
 
         mask_raw, x_raw = {}, {}
-        mask_late = {}
+        mask_grouped, x_grouped = {}, {}
         mask_codes, mask_scales, x_codes, x_scales = {}, {}, {}, {}
         d_grouped, d_codes, d_scales = {}, {}, {}
 
         def load_group(g):
-            mask_raw[g] = raw.tile([P, PASSES, PACK * SLOTS], BF16, name="mask_raw")
-            x_raw[g] = raw.tile([P, PASSES, PACK * M], BF16, name="x_raw")
-            for k in range(PASSES):
-                nc.sync.dma_start(out=mask_raw[g][:, k, :], in_=mask_rows[g, k])
-                nc.sync.dma_start(out=x_raw[g][:, k, :], in_=x_rows[g, k])
+            mask_raw[g] = raw.tile([P, PASSES, PACK, SLOTS], BF16, name="mask_raw")
+            x_raw[g] = raw.tile([P, PASSES, PACK, M], BF16, name="x_raw")
+            if BIG_LOADS and g > 0:
+                nc.sync.dma_start(out=mask_raw[g][:], in_=mask_rows[g])
+                nc.sync.dma_start(out=x_raw[g][:], in_=x_rows[g])
+            else:
+                for k in range(PASSES):
+                    nc.sync.dma_start(out=mask_raw[g][:, k], in_=mask_rows[g][:, k])
+                    nc.sync.dma_start(out=x_raw[g][:, k], in_=x_rows[g][:, k])
 
-        def load_weights():
-            for a in range(E // 4):
-                for q in range(4):
-                    nc.sync.dma_start(
-                        out=wi_planes[32 * q : 32 * q + 16, a, :].bitcast(I32),
-                        in_=wi_scales[4 * a : 4 * a + 4, 4 * q : 4 * q + 4, :].bitcast(I32),
-                    )
-            for a in range(E // 4):
+        def load_scales(a):
+            for q in range(4):
                 nc.sync.dma_start(
-                    out=wi_codes[:, 4 * a : 4 * a + 4, :].bitcast(I32),
-                    in_=wi_words[4 * a : 4 * a + 4].rearrange("e p n t -> p e (n t)").bitcast(I32),
+                    out=wi_planes[32 * q : 32 * q + 16, a, :].bitcast(I32),
+                    in_=wi_scales[4 * a : 4 * a + 4, 4 * q : 4 * q + 4, :].bitcast(I32),
                 )
 
-        def regroup_mask(copy, g, k):
-            tile = grouped.tile([P, SLOTS, PACK], BF16, name="mask_grouped%d" % k, align_bytes=64)
-            copy(
-                out=tile[:].rearrange("p (c i) j -> p c j i", i=4),
-                in_=mask_raw[g][:, k, :].rearrange("p (j c i) -> p c j i", j=PACK, i=4),
+        def load_weights(a):
+            nc.sync.dma_start(
+                out=wi_codes[:, 4 * a : 4 * a + 4, :].bitcast(I32),
+                in_=wi_words[4 * a : 4 * a + 4].rearrange("e p n t -> p e (n t)").bitcast(I32),
             )
-            return tile
 
-        def regroup_x(g, k):
-            tile = grouped.tile([P, PACK, P, PACK], BF16, name="x_grouped%d" % k, align_bytes=64)
-            nc.vector.tensor_copy(
-                out=tile[:].rearrange("p t q j -> p q j t"),
-                in_=x_raw[g][:, k, :].rearrange("p (j q t) -> p q j t", j=PACK, t=PACK),
-            )
-            return tile
-
-        def quantise(tile, words, plane):
-            nc.vector.quantize_mx(out=words.bitcast(FP8X4), scales=plane, in_=tile)
-
-        def scalar_regroup(g):
-            mask_late[g] = regroup_mask(nc.scalar.copy, g, 1)
-
-        def prepare(g):
+        def new_group_tiles(g):
+            for k in range(PASSES):
+                mask_grouped[g, k] = grouped.tile([P, SLOTS, PACK], BF16, name="mask_grouped%d" % k, align_bytes=64)
+                x_grouped[g, k] = grouped.tile([P, PACK, P, PACK], BF16, name="x_grouped%d" % k, align_bytes=64)
             mask_codes[g] = codes.tile([P, PASSES, SLOTS], U32, name="mask_codes", align_bytes=64)
             mask_scales[g] = codes.tile([P, PASSES, SLOTS], U8, name="mask_scales", align_bytes=64)
             x_codes[g] = codes.tile([P, PASSES, M], U32, name="x_codes", align_bytes=64)
             x_scales[g] = codes.tile([P, PASSES, M], U8, name="x_scales", align_bytes=64)
-            mask0 = regroup_mask(nc.vector.tensor_copy, g, 0)
-            x0 = regroup_x(g, 0)
-            quantise(mask0[:].rearrange("p w j -> p (w j)"), mask_codes[g][:, 0, :], mask_scales[g][:, 0, :])
-            x1 = regroup_x(g, 1)
-            quantise(x0[:].rearrange("p t q j -> p (t q j)"), x_codes[g][:, 0, :], x_scales[g][:, 0, :])
-            quantise(mask_late[g][:].rearrange("p w j -> p (w j)"), mask_codes[g][:, 1, :], mask_scales[g][:, 1, :])
-            quantise(x1[:].rearrange("p t q j -> p (t q j)"), x_codes[g][:, 1, :], x_scales[g][:, 1, :])
 
-        def dispatch(g, share):
-            pair, member = divmod(g, 2)
-            if member == 0:
-                d_grouped[pair] = middle.tile([P, E, 2, C, PACK], BF16, name="d_grouped", align_bytes=64)
-            for b in range(BANKS):
-                bank = psum_d.tile([P, PACK, P], F32, name="bank")
-                slots = slice(P * b, P * (b + 1))
-                for t in range(PACK):
-                    cols = slice(P * t, P * (t + 1))
-                    for k in range(PASSES):
-                        nc.tensor.matmul_mx(
-                            out=bank[:, t, :],
-                            lhsT=x_codes[g][:, k, cols].bitcast(FP8X4),
-                            lhsT_scale=x_scales[g][:, k, cols],
-                            rhs=mask_codes[g][:, k, slots].bitcast(FP8X4),
-                            rhs_scale=mask_scales[g][:, k, slots],
-                            start=(k == 0),
-                            stop=(k == PASSES - 1),
-                        )
-                copy = nc.vector.tensor_copy if share and b % 2 == 1 else nc.scalar.copy
-                copy(
-                    out=d_grouped[pair][:, EXPERTS_PER_BANK * b : EXPERTS_PER_BANK * (b + 1), member, :, :],
-                    in_=bank[:].rearrange("p t (e c) -> p e c t", e=EXPERTS_PER_BANK),
-                )
-                if member == 1 and b % 2 == 1:
-                    quantise_dispatched(pair, b // 2)
-
-        def quantise_dispatched(pair, half):
-            if half == 0:
-                d_codes[pair] = middle.tile([P, E * P], U32, name="d_codes", align_bytes=64)
-                d_scales[pair] = middle.tile([P, E * P], U8, name="d_scales", align_bytes=64)
-            cols = slice(HALF * P * half, HALF * P * (half + 1))
-            quantise(
-                d_grouped[pair][:, HALF * half : HALF * (half + 1), :, :, :].rearrange("p e g c t -> p (e g c t)"),
-                d_codes[pair][:, cols],
-                d_scales[pair][:, cols],
+        def regroup_mask(copy, g, k, w0, w1):
+            copy(
+                out=mask_grouped[g, k][:, w0:w1, :].rearrange("p (c i) j -> p c j i", i=4),
+                in_=mask_raw[g][:, k, :, w0:w1].rearrange("p j (c i) -> p c j i", i=4),
             )
 
-        def project(pair, half, share):
-            for e in range(HALF * half, HALF * (half + 1)):
-                cols = slice(P * e, P * (e + 1))
-                acc = psum_h.tile([P, H], F32, name="acc")
-                nc.tensor.matmul_mx(
-                    out=acc[:],
-                    lhsT=d_codes[pair][:, cols].bitcast(FP8X4),
-                    lhsT_scale=d_scales[pair][:, cols],
-                    rhs=wi_codes[:, e, :].bitcast(FP8X4),
-                    rhs_scale=wi_planes[4 * (e % 4) : P, e // 4, :],
-                    start=True,
-                    stop=True,
+        def regroup_x(copy, g, k, q0, q1):
+            copy(
+                out=x_grouped[g, k][:, :, q0:q1, :].rearrange("p t q j -> p q j t"),
+                in_=x_raw[g][:, k, :, PACK * q0 : PACK * q1].rearrange("p j (q t) -> p q j t", t=PACK),
+            )
+
+        def quantise_mask(g, k, w0, w1):
+            nc.vector.quantize_mx(
+                out=mask_codes[g][:, k, w0:w1].bitcast(FP8X4),
+                scales=mask_scales[g][:, k, w0:w1],
+                in_=mask_grouped[g, k][:, w0:w1, :].rearrange("p w j -> p (w j)"),
+            )
+
+        def quantise_x(g, k):
+            nc.vector.quantize_mx(
+                out=x_codes[g][:, k, :].bitcast(FP8X4),
+                scales=x_scales[g][:, k, :],
+                in_=x_grouped[g, k][:].rearrange("p t q j -> p (t q j)"),
+            )
+
+        def w_scalar(g):
+            return 0 if (FINE_TAIL and g == G - 1) else W_SCALAR
+
+        def early_regroup(g):
+            new_group_tiles(g)
+            rows = mask_raw[g][:, 1].rearrange("p j w -> p w j")
+            if not PE_REGROUP:
+                regroup_mask(nc.scalar.copy, g, 1, 0, SLOTS)
+            for half in range(2 if PE_REGROUP else 0):
+                bank = psum_r.tile([P, 2, P, PACK], BF16, name="regroup_bank")
+                for u in range(2):
+                    w0 = P * (2 * half + u)
+                    nc.tensor.matmul(out=bank[:, u, :, :], lhsT=ident[:], rhs=rows[:, w0 : w0 + P, :], start=True, stop=True)
+                nc.scalar.copy(
+                    out=mask_grouped[g, 1][:, 2 * P * half : 2 * P * (half + 1), :].rearrange("p w j -> p (w j)"),
+                    in_=bank[:].rearrange("p u w j -> p (u w j)"),
                 )
-                res = results.tile([P, H], F32, name="res")
-                if share and e % 2 == 1:
-                    nc.vector.tensor_scalar_max(out=res[:], in0=acc[:], scalar1=0.0)
-                else:
-                    nc.scalar.activation(out=res[:], in_=acc[:], func=RELU)
+            if Q_BY_GROUP[g]:
+                regroup_x(nc.scalar.copy, g, 1, P - Q_BY_GROUP[g], P)
+            if w_scalar(g):
+                regroup_mask(nc.scalar.copy, g, 0, SLOTS - w_scalar(g), SLOTS)
+
+        def vector_x1(g):
+            if Q_BY_GROUP[g] < P:
+                regroup_x(nc.vector.tensor_copy, g, 1, 0, P - Q_BY_GROUP[g])
+
+        def prepare(g):
+            regroup_mask(nc.vector.tensor_copy, g, 0, 0, SLOTS - w_scalar(g))
+            regroup_x(nc.vector.tensor_copy, g, 0, 0, P)
+            quantise_mask(g, 0, 0, SLOTS)
+            vector_x1(g)
+            quantise_x(g, 0)
+            quantise_mask(g, 1, 0, SLOTS)
+            quantise_x(g, 1)
+
+        def prepare_x(g):
+            regroup_x(nc.vector.tensor_copy, g, 0, 0, P)
+            vector_x1(g)
+            quantise_x(g, 0)
+            quantise_x(g, 1)
+
+        def prepare_mask_bank(g, b):
+            regroup_mask(nc.vector.tensor_copy, g, 0, P * b, P * (b + 1))
+            quantise_mask(g, 1, P * b, P * (b + 1))
+            quantise_mask(g, 0, P * b, P * (b + 1))
+
+        def dispatch_bank(g, b, copy):
+            pair, member = divmod(g, 2)
+            if member == 0 and b == 0:
+                d_grouped[pair] = middle.tile([P, E, 2, C, PACK], BF16, name="d_grouped", align_bytes=64)
+                d_codes[pair] = middle.tile([P, E * P], U32, name="d_codes", align_bytes=64)
+                d_scales[pair] = middle.tile([P, E * P], U8, name="d_scales", align_bytes=64)
+            bank = psum_d.tile([P, PACK, P], F32, name="bank")
+            slots = slice(P * b, P * (b + 1))
+            for t in range(PACK):
+                cols = slice(P * t, P * (t + 1))
+                for k in range(PASSES):
+                    nc.tensor.matmul_mx(
+                        out=bank[:, t, :],
+                        lhsT=x_codes[g][:, k, cols].bitcast(FP8X4),
+                        lhsT_scale=x_scales[g][:, k, cols],
+                        rhs=mask_codes[g][:, k, slots].bitcast(FP8X4),
+                        rhs_scale=mask_scales[g][:, k, slots],
+                        start=(k == 0),
+                        stop=(k == PASSES - 1),
+                    )
+            if copy is None:
+                return bank
+            empty_bank(g, b, bank, copy)
+            return None
+
+        def empty_bank(g, b, bank, copy):
+            pair, member = divmod(g, 2)
+            copy(
+                out=d_grouped[pair][:, EXPERTS_PER_BANK * b : EXPERTS_PER_BANK * (b + 1), member, :, :],
+                in_=bank[:].rearrange("p t (e c) -> p e c t", e=EXPERTS_PER_BANK),
+            )
+
+        def quantise_dispatched(pair, e0, e1):
+            nc.vector.quantize_mx(
+                out=d_codes[pair][:, P * e0 : P * e1].bitcast(FP8X4),
+                scales=d_scales[pair][:, P * e0 : P * e1],
+                in_=d_grouped[pair][:, e0:e1, :, :, :].rearrange("p e g c t -> p (e g c t)"),
+            )
+
+        def project(pair, e0, e1, store_n, share):
+            for s0 in range(e0, e1, store_n):
+                res = results.tile([P, store_n, H], F32, name="res%d" % store_n, bufs=(RES_BUFS if store_n == STORE_N else LAST_BUFS))
+                for e in range(s0, s0 + store_n):
+                    cols = slice(P * e, P * (e + 1))
+                    acc = psum_h.tile([P, H], F32, name="acc")
+                    nc.tensor.matmul_mx(
+                        out=acc[:],
+                        lhsT=d_codes[pair][:, cols].bitcast(FP8X4),
+                        lhsT_scale=d_scales[pair][:, cols],
+                        rhs=wi_codes[:, e, :].bitcast(FP8X4),
+                        rhs_scale=wi_planes[4 * (e % 4) : P, e // 4, :],
+                        start=True,
+                        stop=True,
+                    )
+                    if share and e % 2 == 1:
+                        nc.vector.tensor_scalar_max(out=res[:, e - s0, :], in0=acc[:], scalar1=0.0)
+                    else:
+                        nc.scalar.activation(out=res[:, e - s0, :], in_=acc[:], func=RELU)
                 nc.sync.dma_start(
-                    out=out[e, 2 * pair : 2 * pair + 2, :, :].rearrange("g c h -> (g c) h"), in_=res[:]
+                    out=out[s0 : s0 + store_n, 2 * pair : 2 * pair + 2, :, :].rearrange("e g c h -> (g c) e h"), in_=res[:]
                 )
+
+        def load_step(g):
+            load_group(g)
+            for a in range(2):
+                if g + 1 == SCALES_AFTER[a]:
+                    load_scales(a)
+            for a in range(2):
+                if g + 1 == W_AFTER[a]:
+                    load_weights(a)
 
         nc.vector.memset(wi_planes[:].bitcast(I32), 0)
+        make_identity(nc, ident[:])
         for g in range(LOOKAHEAD):
-            load_group(g)
-        load_weights()
-        scalar_regroup(0)
+            load_step(g)
+        early_regroup(0)
 
+        last = G - 1
         for step in range(G + 2):
-            share = step >= G
+            share = step >= LATE_SHARE_STEP
             if step + LOOKAHEAD < G:
-                load_group(step + LOOKAHEAD)
+                load_step(step + LOOKAHEAD)
+            fine = FINE_TAIL and step == last
             if step < G:
-                prepare(step)
-            if 1 <= step <= G:
-                dispatch(step - 1, share)
+                if fine:
+                    prepare_x(step)
+                else:
+                    prepare(step)
+            if 1 <= step <= G and not (FINE_TAIL and step == G):
+                g = step - 1
+                for b in range(BANKS):
+                    dispatch_bank(g, b, nc.vector.tensor_copy if share and b % 2 == 1 else nc.scalar.copy)
+                    if g % 2 == 1 and b % 2 == 1:
+                        quantise_dispatched(g // 2, HALF * (b // 2), HALF * (b // 2 + 1))
             if step + 1 < G:
-                scalar_regroup(step + 1)
+                early_regroup(step + 1)
             if step >= 2:
                 pair, half = divmod(step - 2, 2)
-                project(pair, half, share)
+                if not (FINE_TAIL and step >= last):
+                    project(pair, HALF * half, HALF * (half + 1), STORE_N if pair < PAIRS - 1 else 1, share)
+            if fine:
+                banks = {}
+                for b in range(BANKS + TAIL_LAG):
+                    if b < BANKS:
+                        prepare_mask_bank(last, b)
+                        banks[b] = dispatch_bank(last, b, None)
+                        project(PAIRS - 2, HALF + b, HALF + b + 1, 1, False)
+                    if 0 <= b - E_LAG < BANKS:
+                        empty_bank(last, b - E_LAG, banks[b - E_LAG], nc.vector.tensor_copy if TAIL_E_VECTOR else nc.scalar.copy)
+                    if b >= TAIL_LAG:
+                        d = b - TAIL_LAG
+                        quantise_dispatched(PAIRS - 1, EXPERTS_PER_BANK * d, EXPERTS_PER_BANK * (d + 1))
+                        project(PAIRS - 1, EXPERTS_PER_BANK * d, EXPERTS_PER_BANK * (d + 1), 1, TAIL_R_SHARE)

@@ -40,6 +40,9 @@ TAIL_LAG = 2
 E_LAG = 1
 TAIL_E_VECTOR = True
 TAIL_R_SHARE = False
+V_LAST_RELUS = 0
+SCALES_WITH_W = True
+FIRST_PROJECT_STEP = 2
 LATE_SHARE_STEP = 8
 HEAD_SPLIT = 1
 
@@ -231,7 +234,7 @@ def tile_flaxpositionwisemoelayer_pa_t_e_kernel(tc, dispatch_mask, x, wi_words, 
                         start=True,
                         stop=True,
                     )
-                    if share and e % 2 == 1:
+                    if (share and e % 2 == 1) or (pair == PAIRS - 1 and FINE_TAIL and e >= E - V_LAST_RELUS):
                         nc.vector.tensor_scalar_max(out=res[:, e - s0, :], in0=acc[:], scalar1=0.0)
                     else:
                         nc.scalar.activation(out=res[:, e - s0, :], in_=acc[:], func=RELU)
@@ -242,10 +245,12 @@ def tile_flaxpositionwisemoelayer_pa_t_e_kernel(tc, dispatch_mask, x, wi_words, 
         def load_step(g):
             load_group(g)
             for a in range(2):
-                if g + 1 == SCALES_AFTER[a]:
+                if g + 1 == SCALES_AFTER[a] and not SCALES_WITH_W:
                     load_scales(a)
             for a in range(2):
                 if g + 1 == W_AFTER[a]:
+                    if SCALES_WITH_W:
+                        load_scales(a)
                     load_weights(a)
 
         nc.vector.memset(wi_planes[:].bitcast(I32), 0)
@@ -273,10 +278,11 @@ def tile_flaxpositionwisemoelayer_pa_t_e_kernel(tc, dispatch_mask, x, wi_words, 
                         quantise_dispatched(g // 2, HALF * (b // 2), HALF * (b // 2 + 1))
             if step + 1 < G:
                 early_regroup(step + 1)
-            if step >= 2:
-                pair, half = divmod(step - 2, 2)
-                if not (FINE_TAIL and step >= last):
-                    project(pair, HALF * half, HALF * (half + 1), STORE_N if pair < PAIRS - 1 else 1, share)
+            for h in range(2 * PAIRS):
+                if max(h + 2, FIRST_PROJECT_STEP) == step:
+                    pair, half = divmod(h, 2)
+                    if not (FINE_TAIL and step >= last):
+                        project(pair, HALF * half, HALF * (half + 1), STORE_N if pair < PAIRS - 1 else 1, share)
             if fine:
                 banks = {}
                 for b in range(BANKS + TAIL_LAG):

@@ -1,7 +1,6 @@
 from contextlib import ExitStack
 
 import concourse.mybir as mybir
-from concourse.masks import make_identity
 
 BF16 = mybir.dt.bfloat16
 F32 = mybir.dt.float32
@@ -18,57 +17,37 @@ K_PASS = P * PACK
 PASSES = S // K_PASS
 SLOTS = E * C
 PAIRS = G // 2
-EXPERTS_PER_BANK = P // C
+BANK_EXPERTS = P // C
 BANKS = SLOTS // P
 HALF = E // 2
-
+RUN = 4
 LOOKAHEAD = 4
-RAW_BUFS = 6
-Q_BY_GROUP = (0, 0, 0, 0, 0, 0, 0, 0)
-D_BANKS, H_BANKS, R_BANKS = 4, 4, 0
-PE_REGROUP = False
-W_SCALAR = 0
-HEAD_PIECES = 1
-BIG_LOADS = False
-STORE_N = 1
-RES_BUFS = 12
-LAST_BUFS = 12
-W_AFTER = (4, 4)
-SCALES_AFTER = (4, 4)
-FINE_TAIL = True
-TAIL_LAG = 2
-E_LAG = 1
-TAIL_E_VECTOR = True
-TAIL_R_SHARE = False
-V_LAST_RELUS = 0
-SCALES_WITH_W = True
-FIRST_PROJECT_STEP = 2
-LATE_SHARE_STEP = 8
-HEAD_SPLIT = 1
+LAST = G - 1
+EMPTY_LAG = 1
+QUANTISE_LAG = 2
 
 FLOPS = 2 * G * S * SLOTS * M + 2 * E * G * C * M * H
 
 
 def tile_flaxpositionwisemoelayer_pa_t_e_kernel(tc, dispatch_mask, x, wi_words, wi_scales, out):
     nc = tc.nc
+
     mask_rows = dispatch_mask.rearrange("g (k p j) e c -> g p k j (e c)", k=PASSES, p=P, j=PACK)
     x_rows = x.rearrange("g (k p j) m -> g p k j m", k=PASSES, p=P, j=PACK)
 
     with ExitStack() as ctx:
         consts = ctx.enter_context(tc.tile_pool(name="consts", bufs=1))
-        raw = ctx.enter_context(tc.tile_pool(name="raw", bufs=RAW_BUFS))
+        raw = ctx.enter_context(tc.tile_pool(name="raw", bufs=LOOKAHEAD + 2))
         grouped = ctx.enter_context(tc.tile_pool(name="grouped", bufs=2))
         codes = ctx.enter_context(tc.tile_pool(name="codes", bufs=3))
         middle = ctx.enter_context(tc.tile_pool(name="middle", bufs=2))
-        results = ctx.enter_context(tc.tile_pool(name="results", bufs=RES_BUFS))
-        psum_d = ctx.enter_context(tc.psum_pool(name="psum_d", bufs=D_BANKS))
-        psum_h = ctx.enter_context(tc.psum_pool(name="psum_h", bufs=H_BANKS))
-        psum_r = ctx.enter_context(tc.psum_pool(name="psum_r", bufs=max(R_BANKS, 1)))
+        results = ctx.enter_context(tc.tile_pool(name="results", bufs=3 * HALF))
+        psum_d = ctx.enter_context(tc.psum_pool(name="psum_d", bufs=BANKS))
+        psum_h = ctx.enter_context(tc.psum_pool(name="psum_h", bufs=HALF))
         ctx.enter_context(tc.manual_schedule())
 
         wi_codes = consts.tile([P, E, H], U32, name="wi_codes", align_bytes=64)
-        wi_planes = consts.tile([P, E // 4, H], U8, name="wi_planes", align_bytes=64)
-        ident = consts.tile([P, P], BF16, name="ident")
+        wi_planes = consts.tile([P, E // HALF, H], U8, name="wi_planes", align_bytes=64)
 
         mask_raw, x_raw = {}, {}
         mask_grouped, x_grouped = {}, {}
@@ -78,46 +57,32 @@ def tile_flaxpositionwisemoelayer_pa_t_e_kernel(tc, dispatch_mask, x, wi_words, 
         def load_group(g):
             mask_raw[g] = raw.tile([P, PASSES, PACK, SLOTS], BF16, name="mask_raw")
             x_raw[g] = raw.tile([P, PASSES, PACK, M], BF16, name="x_raw")
-            if BIG_LOADS and g > 0:
-                nc.sync.dma_start(out=mask_raw[g][:], in_=mask_rows[g])
-                nc.sync.dma_start(out=x_raw[g][:], in_=x_rows[g])
-            else:
-                for k in range(PASSES):
-                    nc.sync.dma_start(out=mask_raw[g][:, k], in_=mask_rows[g][:, k])
-                    nc.sync.dma_start(out=x_raw[g][:, k], in_=x_rows[g][:, k])
+            for k in range(PASSES):
+                nc.sync.dma_start(out=mask_raw[g][:, k], in_=mask_rows[g][:, k])
+                nc.sync.dma_start(out=x_raw[g][:, k], in_=x_rows[g][:, k])
 
-        def load_scales(a):
+        def load_weights(a):
+            experts = slice(HALF * a, HALF * (a + 1))
             for q in range(4):
                 nc.sync.dma_start(
                     out=wi_planes[32 * q : 32 * q + 16, a, :].bitcast(I32),
-                    in_=wi_scales[4 * a : 4 * a + 4, 4 * q : 4 * q + 4, :].bitcast(I32),
+                    in_=wi_scales[experts, 4 * q : 4 * q + 4, :].bitcast(I32),
                 )
-
-        def load_weights(a):
             nc.sync.dma_start(
-                out=wi_codes[:, 4 * a : 4 * a + 4, :].bitcast(I32),
-                in_=wi_words[4 * a : 4 * a + 4].rearrange("e p n t -> p e (n t)").bitcast(I32),
+                out=wi_codes[:, experts, :].bitcast(I32),
+                in_=wi_words[experts].rearrange("e p n t -> p e (n t)").bitcast(I32),
             )
-
-        def new_group_tiles(g):
-            for k in range(PASSES):
-                mask_grouped[g, k] = grouped.tile([P, SLOTS, PACK], BF16, name="mask_grouped%d" % k, align_bytes=64)
-                x_grouped[g, k] = grouped.tile([P, PACK, P, PACK], BF16, name="x_grouped%d" % k, align_bytes=64)
-            mask_codes[g] = codes.tile([P, PASSES, SLOTS], U32, name="mask_codes", align_bytes=64)
-            mask_scales[g] = codes.tile([P, PASSES, SLOTS], U8, name="mask_scales", align_bytes=64)
-            x_codes[g] = codes.tile([P, PASSES, M], U32, name="x_codes", align_bytes=64)
-            x_scales[g] = codes.tile([P, PASSES, M], U8, name="x_scales", align_bytes=64)
 
         def regroup_mask(copy, g, k, w0, w1):
             copy(
-                out=mask_grouped[g, k][:, w0:w1, :].rearrange("p (c i) j -> p c j i", i=4),
-                in_=mask_raw[g][:, k, :, w0:w1].rearrange("p j (c i) -> p c j i", i=4),
+                out=mask_grouped[g, k][:, w0:w1, :].rearrange("p (c i) j -> p c j i", i=RUN),
+                in_=mask_raw[g][:, k, :, w0:w1].rearrange("p j (c i) -> p c j i", i=RUN),
             )
 
-        def regroup_x(copy, g, k, q0, q1):
-            copy(
-                out=x_grouped[g, k][:, :, q0:q1, :].rearrange("p t q j -> p q j t"),
-                in_=x_raw[g][:, k, :, PACK * q0 : PACK * q1].rearrange("p j (q t) -> p q j t", t=PACK),
+        def regroup_x(g, k):
+            nc.vector.tensor_copy(
+                out=x_grouped[g, k][:].rearrange("p t q j -> p q j t"),
+                in_=x_raw[g][:, k].rearrange("p j (q t) -> p q j t", t=PACK),
             )
 
         def quantise_mask(g, k, w0, w1):
@@ -134,44 +99,28 @@ def tile_flaxpositionwisemoelayer_pa_t_e_kernel(tc, dispatch_mask, x, wi_words, 
                 in_=x_grouped[g, k][:].rearrange("p t q j -> p (t q j)"),
             )
 
-        def w_scalar(g):
-            return 0 if (FINE_TAIL and g == G - 1) else W_SCALAR
-
-        def early_regroup(g):
-            new_group_tiles(g)
-            rows = mask_raw[g][:, 1].rearrange("p j w -> p w j")
-            if not PE_REGROUP:
-                regroup_mask(nc.scalar.copy, g, 1, 0, SLOTS)
-            for half in range(2 if PE_REGROUP else 0):
-                bank = psum_r.tile([P, 2, P, PACK], BF16, name="regroup_bank")
-                for u in range(2):
-                    w0 = P * (2 * half + u)
-                    nc.tensor.matmul(out=bank[:, u, :, :], lhsT=ident[:], rhs=rows[:, w0 : w0 + P, :], start=True, stop=True)
-                nc.scalar.copy(
-                    out=mask_grouped[g, 1][:, 2 * P * half : 2 * P * (half + 1), :].rearrange("p w j -> p (w j)"),
-                    in_=bank[:].rearrange("p u w j -> p (u w j)"),
-                )
-            if Q_BY_GROUP[g]:
-                regroup_x(nc.scalar.copy, g, 1, P - Q_BY_GROUP[g], P)
-            if w_scalar(g):
-                regroup_mask(nc.scalar.copy, g, 0, SLOTS - w_scalar(g), SLOTS)
-
-        def vector_x1(g):
-            if Q_BY_GROUP[g] < P:
-                regroup_x(nc.vector.tensor_copy, g, 1, 0, P - Q_BY_GROUP[g])
+        def scalar_regroup(g):
+            for k in range(PASSES):
+                mask_grouped[g, k] = grouped.tile([P, SLOTS, PACK], BF16, name="mask_grouped%d" % k, align_bytes=64)
+                x_grouped[g, k] = grouped.tile([P, PACK, P, PACK], BF16, name="x_grouped%d" % k, align_bytes=64)
+            mask_codes[g] = codes.tile([P, PASSES, SLOTS], U32, name="mask_codes", align_bytes=64)
+            mask_scales[g] = codes.tile([P, PASSES, SLOTS], U8, name="mask_scales", align_bytes=64)
+            x_codes[g] = codes.tile([P, PASSES, M], U32, name="x_codes", align_bytes=64)
+            x_scales[g] = codes.tile([P, PASSES, M], U8, name="x_scales", align_bytes=64)
+            regroup_mask(nc.scalar.copy, g, 1, 0, SLOTS)
 
         def prepare(g):
-            regroup_mask(nc.vector.tensor_copy, g, 0, 0, SLOTS - w_scalar(g))
-            regroup_x(nc.vector.tensor_copy, g, 0, 0, P)
+            regroup_mask(nc.vector.tensor_copy, g, 0, 0, SLOTS)
+            regroup_x(g, 0)
             quantise_mask(g, 0, 0, SLOTS)
-            vector_x1(g)
+            regroup_x(g, 1)
             quantise_x(g, 0)
             quantise_mask(g, 1, 0, SLOTS)
             quantise_x(g, 1)
 
         def prepare_x(g):
-            regroup_x(nc.vector.tensor_copy, g, 0, 0, P)
-            vector_x1(g)
+            regroup_x(g, 0)
+            regroup_x(g, 1)
             quantise_x(g, 0)
             quantise_x(g, 1)
 
@@ -180,7 +129,7 @@ def tile_flaxpositionwisemoelayer_pa_t_e_kernel(tc, dispatch_mask, x, wi_words, 
             quantise_mask(g, 1, P * b, P * (b + 1))
             quantise_mask(g, 0, P * b, P * (b + 1))
 
-        def dispatch_bank(g, b, copy):
+        def dispatch_bank(g, b):
             pair, member = divmod(g, 2)
             if member == 0 and b == 0:
                 d_grouped[pair] = middle.tile([P, E, 2, C, PACK], BF16, name="d_grouped", align_bytes=64)
@@ -200,16 +149,13 @@ def tile_flaxpositionwisemoelayer_pa_t_e_kernel(tc, dispatch_mask, x, wi_words, 
                         start=(k == 0),
                         stop=(k == PASSES - 1),
                     )
-            if copy is None:
-                return bank
-            empty_bank(g, b, bank, copy)
-            return None
+            return bank
 
-        def empty_bank(g, b, bank, copy):
+        def empty_bank(copy, g, b, bank):
             pair, member = divmod(g, 2)
             copy(
-                out=d_grouped[pair][:, EXPERTS_PER_BANK * b : EXPERTS_PER_BANK * (b + 1), member, :, :],
-                in_=bank[:].rearrange("p t (e c) -> p e c t", e=EXPERTS_PER_BANK),
+                out=d_grouped[pair][:, BANK_EXPERTS * b : BANK_EXPERTS * (b + 1), member, :, :],
+                in_=bank[:].rearrange("p t (e c) -> p e c t", e=BANK_EXPERTS),
             )
 
         def quantise_dispatched(pair, e0, e1):
@@ -219,80 +165,58 @@ def tile_flaxpositionwisemoelayer_pa_t_e_kernel(tc, dispatch_mask, x, wi_words, 
                 in_=d_grouped[pair][:, e0:e1, :, :, :].rearrange("p e g c t -> p (e g c t)"),
             )
 
-        def project(pair, e0, e1, store_n, share):
-            for s0 in range(e0, e1, store_n):
-                res = results.tile([P, store_n, H], F32, name="res%d" % store_n, bufs=(RES_BUFS if store_n == STORE_N else LAST_BUFS))
-                for e in range(s0, s0 + store_n):
-                    cols = slice(P * e, P * (e + 1))
-                    acc = psum_h.tile([P, H], F32, name="acc")
-                    nc.tensor.matmul_mx(
-                        out=acc[:],
-                        lhsT=d_codes[pair][:, cols].bitcast(FP8X4),
-                        lhsT_scale=d_scales[pair][:, cols],
-                        rhs=wi_codes[:, e, :].bitcast(FP8X4),
-                        rhs_scale=wi_planes[4 * (e % 4) : P, e // 4, :],
-                        start=True,
-                        stop=True,
-                    )
-                    if (share and e % 2 == 1) or (pair == PAIRS - 1 and FINE_TAIL and e >= E - V_LAST_RELUS):
-                        nc.vector.tensor_scalar_max(out=res[:, e - s0, :], in0=acc[:], scalar1=0.0)
-                    else:
-                        nc.scalar.activation(out=res[:, e - s0, :], in_=acc[:], func=RELU)
-                nc.sync.dma_start(
-                    out=out[s0 : s0 + store_n, 2 * pair : 2 * pair + 2, :, :].rearrange("e g c h -> (g c) e h"), in_=res[:]
-                )
-
-        def load_step(g):
-            load_group(g)
-            for a in range(2):
-                if g + 1 == SCALES_AFTER[a] and not SCALES_WITH_W:
-                    load_scales(a)
-            for a in range(2):
-                if g + 1 == W_AFTER[a]:
-                    if SCALES_WITH_W:
-                        load_scales(a)
-                    load_weights(a)
+        def project(pair, e):
+            cols = slice(P * e, P * (e + 1))
+            acc = psum_h.tile([P, H], F32, name="acc")
+            nc.tensor.matmul_mx(
+                out=acc[:],
+                lhsT=d_codes[pair][:, cols].bitcast(FP8X4),
+                lhsT_scale=d_scales[pair][:, cols],
+                rhs=wi_codes[:, e, :].bitcast(FP8X4),
+                rhs_scale=wi_planes[4 * (e % HALF) : P, e // HALF, :],
+                start=True,
+                stop=True,
+            )
+            res = results.tile([P, H], F32, name="res")
+            nc.scalar.activation(out=res[:], in_=acc[:], func=RELU)
+            nc.sync.dma_start(out=out[e, 2 * pair : 2 * pair + 2, :, :].rearrange("g c h -> (g c) h"), in_=res[:])
 
         nc.vector.memset(wi_planes[:].bitcast(I32), 0)
-        make_identity(nc, ident[:])
         for g in range(LOOKAHEAD):
-            load_step(g)
-        early_regroup(0)
+            load_group(g)
+        for a in range(E // HALF):
+            load_weights(a)
+        scalar_regroup(0)
 
-        last = G - 1
-        for step in range(G + 2):
-            share = step >= LATE_SHARE_STEP
+        for step in range(LAST):
             if step + LOOKAHEAD < G:
-                load_step(step + LOOKAHEAD)
-            fine = FINE_TAIL and step == last
-            if step < G:
-                if fine:
-                    prepare_x(step)
-                else:
-                    prepare(step)
-            if 1 <= step <= G and not (FINE_TAIL and step == G):
+                load_group(step + LOOKAHEAD)
+            prepare(step)
+            if step >= 1:
                 g = step - 1
                 for b in range(BANKS):
-                    dispatch_bank(g, b, nc.vector.tensor_copy if share and b % 2 == 1 else nc.scalar.copy)
+                    empty_bank(nc.scalar.copy, g, b, dispatch_bank(g, b))
                     if g % 2 == 1 and b % 2 == 1:
                         quantise_dispatched(g // 2, HALF * (b // 2), HALF * (b // 2 + 1))
-            if step + 1 < G:
-                early_regroup(step + 1)
-            for h in range(2 * PAIRS):
-                if max(h + 2, FIRST_PROJECT_STEP) == step:
-                    pair, half = divmod(h, 2)
-                    if not (FINE_TAIL and step >= last):
-                        project(pair, HALF * half, HALF * (half + 1), STORE_N if pair < PAIRS - 1 else 1, share)
-            if fine:
-                banks = {}
-                for b in range(BANKS + TAIL_LAG):
-                    if b < BANKS:
-                        prepare_mask_bank(last, b)
-                        banks[b] = dispatch_bank(last, b, None)
-                        project(PAIRS - 2, HALF + b, HALF + b + 1, 1, False)
-                    if 0 <= b - E_LAG < BANKS:
-                        empty_bank(last, b - E_LAG, banks[b - E_LAG], nc.vector.tensor_copy if TAIL_E_VECTOR else nc.scalar.copy)
-                    if b >= TAIL_LAG:
-                        d = b - TAIL_LAG
-                        quantise_dispatched(PAIRS - 1, EXPERTS_PER_BANK * d, EXPERTS_PER_BANK * (d + 1))
-                        project(PAIRS - 1, EXPERTS_PER_BANK * d, EXPERTS_PER_BANK * (d + 1), 1, TAIL_R_SHARE)
+            scalar_regroup(step + 1)
+            if step >= 2:
+                pair, half = divmod(step - 2, 2)
+                for e in range(HALF * half, HALF * (half + 1)):
+                    project(pair, e)
+
+        prepare_x(LAST)
+        for b in range(BANKS):
+            empty_bank(nc.scalar.copy, LAST - 1, b, dispatch_bank(LAST - 1, b))
+        banks = {}
+        for b in range(BANKS + QUANTISE_LAG):
+            if b < BANKS:
+                prepare_mask_bank(LAST, b)
+                banks[b] = dispatch_bank(LAST, b)
+                project(PAIRS - 2, HALF + b)
+            if 0 <= b - EMPTY_LAG < BANKS:
+                empty_bank(nc.vector.tensor_copy, LAST, b - EMPTY_LAG, banks[b - EMPTY_LAG])
+            if b >= QUANTISE_LAG:
+                e0 = BANK_EXPERTS * (b - QUANTISE_LAG)
+                quantise_dispatched(PAIRS - 1, e0, e0 + BANK_EXPERTS)
+                for e in range(e0, e0 + BANK_EXPERTS):
+                    project(PAIRS - 1, e)

@@ -54,12 +54,21 @@ def tile_flaxpositionwisemoelayer_pa_t_e_kernel(tc, dispatch_mask, x, wi_words, 
         mask_codes, mask_scales, x_codes, x_scales = {}, {}, {}, {}
         d_grouped, d_codes, d_scales = {}, {}, {}
 
+        def load_mask(g, k):
+            nc.sync.dma_start(out=mask_raw[g][:, k], in_=mask_rows[g][:, k])
+
         def load_group(g):
-            mask_raw[g] = raw.tile([P, PASSES, PACK, SLOTS], BF16, name="mask_raw")
             x_raw[g] = raw.tile([P, PASSES, PACK, M], BF16, name="x_raw")
-            for k in range(PASSES):
-                nc.sync.dma_start(out=mask_raw[g][:, k], in_=mask_rows[g][:, k])
-                nc.sync.dma_start(out=x_raw[g][:, k], in_=x_rows[g][:, k])
+            if g == 0:
+                mask_raw[g] = raw.tile([P, PASSES, PACK, SLOTS], BF16, name="mask_raw")
+            load_mask(g, 0)
+            nc.sync.dma_start(out=x_raw[g][:, 0], in_=x_rows[g][:, 0])
+            if g == 0:
+                load_mask(g, 1)
+            nc.sync.dma_start(out=x_raw[g][:, 1], in_=x_rows[g][:, 1])
+            if g + 1 < G:
+                mask_raw[g + 1] = raw.tile([P, PASSES, PACK, SLOTS], BF16, name="mask_raw")
+                load_mask(g + 1, 1)
 
         def load_weights(a):
             experts = slice(HALF * a, HALF * (a + 1))
@@ -184,8 +193,8 @@ def tile_flaxpositionwisemoelayer_pa_t_e_kernel(tc, dispatch_mask, x, wi_words, 
         nc.vector.memset(wi_planes[:].bitcast(I32), 0)
         for g in range(LOOKAHEAD):
             load_group(g)
-        for a in range(E // HALF):
-            load_weights(a)
+            if g >= LOOKAHEAD - E // HALF:
+                load_weights(g - (LOOKAHEAD - E // HALF))
         scalar_regroup(0)
 
         for step in range(LAST):

@@ -23,8 +23,7 @@ HALF = E // 2
 RUN = 4
 LOOKAHEAD = 4
 LAST = G - 1
-EMPTY_LAG = 1
-QUANTISE_LAG = 2
+BANK_LAG = 1
 
 FLOPS = 2 * G * S * SLOTS * M + 2 * E * G * C * M * H
 
@@ -41,7 +40,7 @@ def tile_flaxpositionwisemoelayer_pa_t_e_kernel(tc, dispatch_mask, x, wi_words, 
         grouped = ctx.enter_context(tc.tile_pool(name="grouped", bufs=2))
         codes = ctx.enter_context(tc.tile_pool(name="codes", bufs=3))
         middle = ctx.enter_context(tc.tile_pool(name="middle", bufs=2))
-        results = ctx.enter_context(tc.tile_pool(name="results", bufs=3 * HALF))
+        results = ctx.enter_context(tc.tile_pool(name="results", bufs=3 * HALF // BANK_EXPERTS))
         psum_d = ctx.enter_context(tc.psum_pool(name="psum_d", bufs=BANKS))
         psum_h = ctx.enter_context(tc.psum_pool(name="psum_h", bufs=HALF))
         ctx.enter_context(tc.manual_schedule())
@@ -53,6 +52,7 @@ def tile_flaxpositionwisemoelayer_pa_t_e_kernel(tc, dispatch_mask, x, wi_words, 
         mask_grouped, x_grouped = {}, {}
         mask_codes, mask_scales, x_codes, x_scales = {}, {}, {}, {}
         d_grouped, d_codes, d_scales = {}, {}, {}
+        res = {}
 
         def load_mask(g, k):
             nc.sync.dma_start(out=mask_raw[g][:, k], in_=mask_rows[g][:, k])
@@ -125,6 +125,9 @@ def tile_flaxpositionwisemoelayer_pa_t_e_kernel(tc, dispatch_mask, x, wi_words, 
             regroup_x(g, 1)
             quantise_x(g, 0)
             quantise_mask(g, 1, 0, SLOTS)
+            if g >= 2 and g % 2 == 0:
+                quantise_dispatched(g // 2 - 1, 0, HALF)
+                quantise_dispatched(g // 2 - 1, HALF, E)
             quantise_x(g, 1)
 
         def prepare_x(g):
@@ -174,7 +177,7 @@ def tile_flaxpositionwisemoelayer_pa_t_e_kernel(tc, dispatch_mask, x, wi_words, 
                 in_=d_grouped[pair][:, e0:e1, :, :, :].rearrange("p e g c t -> p (e g c t)"),
             )
 
-        def project(pair, e):
+        def project(pair, e, together):
             cols = slice(P * e, P * (e + 1))
             acc = psum_h.tile([P, H], F32, name="acc")
             nc.tensor.matmul_mx(
@@ -186,9 +189,17 @@ def tile_flaxpositionwisemoelayer_pa_t_e_kernel(tc, dispatch_mask, x, wi_words, 
                 start=True,
                 stop=True,
             )
-            res = results.tile([P, H], F32, name="res")
-            nc.scalar.activation(out=res[:], in_=acc[:], func=RELU)
-            nc.sync.dma_start(out=out[e, 2 * pair : 2 * pair + 2, :, :].rearrange("g c h -> (g c) h"), in_=res[:])
+            first, place = e - e % BANK_EXPERTS, e % BANK_EXPERTS
+            if place == 0:
+                res[pair] = results.tile([P, BANK_EXPERTS, H], F32, name="res")
+            nc.scalar.activation(out=res[pair][:, place, :], in_=acc[:], func=RELU)
+            groups = slice(2 * pair, 2 * pair + 2)
+            if not together:
+                nc.sync.dma_start(out=out[e, groups, :, :].rearrange("g c h -> (g c) h"), in_=res[pair][:, place, :])
+            elif place == BANK_EXPERTS - 1:
+                nc.sync.dma_start(
+                    out=out[first : e + 1, groups, :, :].rearrange("e g c h -> (g c) e h"), in_=res[pair][:]
+                )
 
         nc.vector.memset(wi_planes[:].bitcast(I32), 0)
         for g in range(LOOKAHEAD):
@@ -200,32 +211,28 @@ def tile_flaxpositionwisemoelayer_pa_t_e_kernel(tc, dispatch_mask, x, wi_words, 
         for step in range(LAST):
             if step + LOOKAHEAD < G:
                 load_group(step + LOOKAHEAD)
-            prepare(step)
             if step >= 1:
-                g = step - 1
                 for b in range(BANKS):
-                    empty_bank(nc.scalar.copy, g, b, dispatch_bank(g, b))
-                    if g % 2 == 1 and b % 2 == 1:
-                        quantise_dispatched(g // 2, HALF * (b // 2), HALF * (b // 2 + 1))
+                    empty_bank(nc.scalar.copy, step - 1, b, dispatch_bank(step - 1, b))
+            prepare(step)
             scalar_regroup(step + 1)
             if step >= 2:
                 pair, half = divmod(step - 2, 2)
                 for e in range(HALF * half, HALF * (half + 1)):
-                    project(pair, e)
+                    project(pair, e, True)
 
         prepare_x(LAST)
         for b in range(BANKS):
             empty_bank(nc.scalar.copy, LAST - 1, b, dispatch_bank(LAST - 1, b))
         banks = {}
-        for b in range(BANKS + QUANTISE_LAG):
+        for b in range(BANKS + BANK_LAG):
             if b < BANKS:
+                project(PAIRS - 2, HALF + b, False)
                 prepare_mask_bank(LAST, b)
                 banks[b] = dispatch_bank(LAST, b)
-                project(PAIRS - 2, HALF + b)
-            if 0 <= b - EMPTY_LAG < BANKS:
-                empty_bank(nc.vector.tensor_copy, LAST, b - EMPTY_LAG, banks[b - EMPTY_LAG])
-            if b >= QUANTISE_LAG:
-                e0 = BANK_EXPERTS * (b - QUANTISE_LAG)
-                quantise_dispatched(PAIRS - 1, e0, e0 + BANK_EXPERTS)
-                for e in range(e0, e0 + BANK_EXPERTS):
-                    project(PAIRS - 1, e)
+            if b >= BANK_LAG:
+                d = b - BANK_LAG
+                empty_bank(nc.vector.tensor_copy, LAST, d, banks[d])
+                quantise_dispatched(PAIRS - 1, BANK_EXPERTS * d, BANK_EXPERTS * (d + 1))
+                for e in range(BANK_EXPERTS * d, BANK_EXPERTS * (d + 1)):
+                    project(PAIRS - 1, e, False)

from contextlib import ExitStack

import concourse.mybir as mybir

BF16 = mybir.dt.bfloat16
F32 = mybir.dt.float32
I32 = mybir.dt.int32
U32 = mybir.dt.uint32
U8 = mybir.dt.uint8
FP8X4 = mybir.dt.float8_e4m3fn_x4
RELU = mybir.ActivationFunctionType.Relu

G, S, M, H, E, C = 8, 1024, 512, 512, 8, 64
P = 128
PACK = 4
K_PASS = P * PACK
PASSES = S // K_PASS
SLOTS = E * C
PAIRS = G // 2
BANK_EXPERTS = P // C
BANKS = SLOTS // P
HALF = E // 2
RUN = 4
LOOKAHEAD = 4
LAST = G - 1
BANK_LAG = 1

FLOPS = 2 * G * S * SLOTS * M + 2 * E * G * C * M * H


def tile_flaxpositionwisemoelayer_pa_t_e_kernel(tc, dispatch_mask, x, wi_words, wi_scales, out):
    nc = tc.nc

    mask_rows = dispatch_mask.rearrange("g (k p j) e c -> g p k j (e c)", k=PASSES, p=P, j=PACK)
    x_rows = x.rearrange("g (k p j) m -> g p k j m", k=PASSES, p=P, j=PACK)

    with ExitStack() as ctx:
        consts = ctx.enter_context(tc.tile_pool(name="consts", bufs=1))
        raw = ctx.enter_context(tc.tile_pool(name="raw", bufs=LOOKAHEAD + 2))
        grouped = ctx.enter_context(tc.tile_pool(name="grouped", bufs=2))
        codes = ctx.enter_context(tc.tile_pool(name="codes", bufs=3))
        middle = ctx.enter_context(tc.tile_pool(name="middle", bufs=2))
        results = ctx.enter_context(tc.tile_pool(name="results", bufs=3 * HALF // BANK_EXPERTS))
        psum_d = ctx.enter_context(tc.psum_pool(name="psum_d", bufs=BANKS))
        psum_h = ctx.enter_context(tc.psum_pool(name="psum_h", bufs=HALF))
        ctx.enter_context(tc.manual_schedule())

        wi_codes = consts.tile([P, E, H], U32, name="wi_codes", align_bytes=64)
        wi_planes = consts.tile([P, E // HALF, H], U8, name="wi_planes", align_bytes=64)

        mask_raw, x_raw = {}, {}
        mask_grouped, x_grouped = {}, {}
        mask_codes, mask_scales, x_codes, x_scales = {}, {}, {}, {}
        d_grouped, d_codes, d_scales = {}, {}, {}
        res = {}

        def load_mask(g, k):
            nc.sync.dma_start(out=mask_raw[g][:, k], in_=mask_rows[g][:, k])

        def load_group(g):
            x_raw[g] = raw.tile([P, PASSES, PACK, M], BF16, name="x_raw")
            if g == 0:
                mask_raw[g] = raw.tile([P, PASSES, PACK, SLOTS], BF16, name="mask_raw")
            load_mask(g, 0)
            nc.sync.dma_start(out=x_raw[g][:, 0], in_=x_rows[g][:, 0])
            if g == 0:
                load_mask(g, 1)
            nc.sync.dma_start(out=x_raw[g][:, 1], in_=x_rows[g][:, 1])
            if g + 1 < G:
                mask_raw[g + 1] = raw.tile([P, PASSES, PACK, SLOTS], BF16, name="mask_raw")
                load_mask(g + 1, 1)

        def load_weights(a):
            experts = slice(HALF * a, HALF * (a + 1))
            for q in range(4):
                nc.sync.dma_start(
                    out=wi_planes[32 * q : 32 * q + 16, a, :].bitcast(I32),
                    in_=wi_scales[experts, 4 * q : 4 * q + 4, :].bitcast(I32),
                )
            nc.sync.dma_start(
                out=wi_codes[:, experts, :].bitcast(I32),
                in_=wi_words[experts].rearrange("e p n t -> p e (n t)").bitcast(I32),
            )

        def regroup_mask(copy, g, k, w0, w1):
            copy(
                out=mask_grouped[g, k][:, w0:w1, :].rearrange("p (c i) j -> p c j i", i=RUN),
                in_=mask_raw[g][:, k, :, w0:w1].rearrange("p j (c i) -> p c j i", i=RUN),
            )

        def regroup_x(g, k):
            nc.vector.tensor_copy(
                out=x_grouped[g, k][:].rearrange("p t q j -> p q j t"),
                in_=x_raw[g][:, k].rearrange("p j (q t) -> p q j t", t=PACK),
            )

        def quantise_mask(g, k, w0, w1):
            nc.vector.quantize_mx(
                out=mask_codes[g][:, k, w0:w1].bitcast(FP8X4),
                scales=mask_scales[g][:, k, w0:w1],
                in_=mask_grouped[g, k][:, w0:w1, :].rearrange("p w j -> p (w j)"),
            )

        def quantise_x(g, k):
            nc.vector.quantize_mx(
                out=x_codes[g][:, k, :].bitcast(FP8X4),
                scales=x_scales[g][:, k, :],
                in_=x_grouped[g, k][:].rearrange("p t q j -> p (t q j)"),
            )

        def scalar_regroup(g):
            for k in range(PASSES):
                mask_grouped[g, k] = grouped.tile([P, SLOTS, PACK], BF16, name="mask_grouped%d" % k, align_bytes=64)
                x_grouped[g, k] = grouped.tile([P, PACK, P, PACK], BF16, name="x_grouped%d" % k, align_bytes=64)
            mask_codes[g] = codes.tile([P, PASSES, SLOTS], U32, name="mask_codes", align_bytes=64)
            mask_scales[g] = codes.tile([P, PASSES, SLOTS], U8, name="mask_scales", align_bytes=64)
            x_codes[g] = codes.tile([P, PASSES, M], U32, name="x_codes", align_bytes=64)
            x_scales[g] = codes.tile([P, PASSES, M], U8, name="x_scales", align_bytes=64)
            regroup_mask(nc.scalar.copy, g, 1, 0, SLOTS)

        def prepare(g):
            regroup_mask(nc.vector.tensor_copy, g, 0, 0, SLOTS)
            regroup_x(g, 0)
            quantise_mask(g, 0, 0, SLOTS)
            regroup_x(g, 1)
            quantise_x(g, 0)
            quantise_mask(g, 1, 0, SLOTS)
            if g >= 2 and g % 2 == 0:
                quantise_dispatched(g // 2 - 1, 0, HALF)
                quantise_dispatched(g // 2 - 1, HALF, E)
            quantise_x(g, 1)

        def prepare_x(g):
            regroup_x(g, 0)
            regroup_x(g, 1)
            quantise_x(g, 0)
            quantise_x(g, 1)

        def prepare_mask_bank(g, b):
            regroup_mask(nc.vector.tensor_copy, g, 0, P * b, P * (b + 1))
            quantise_mask(g, 1, P * b, P * (b + 1))
            quantise_mask(g, 0, P * b, P * (b + 1))

        def dispatch_bank(g, b):
            pair, member = divmod(g, 2)
            if member == 0 and b == 0:
                d_grouped[pair] = middle.tile([P, E, 2, C, PACK], BF16, name="d_grouped", align_bytes=64)
                d_codes[pair] = middle.tile([P, E * P], U32, name="d_codes", align_bytes=64)
                d_scales[pair] = middle.tile([P, E * P], U8, name="d_scales", align_bytes=64)
            bank = psum_d.tile([P, PACK, P], F32, name="bank")
            slots = slice(P * b, P * (b + 1))
            for t in range(PACK):
                cols = slice(P * t, P * (t + 1))
                for k in range(PASSES):
                    nc.tensor.matmul_mx(
                        out=bank[:, t, :],
                        lhsT=x_codes[g][:, k, cols].bitcast(FP8X4),
                        lhsT_scale=x_scales[g][:, k, cols],
                        rhs=mask_codes[g][:, k, slots].bitcast(FP8X4),
                        rhs_scale=mask_scales[g][:, k, slots],
                        start=(k == 0),
                        stop=(k == PASSES - 1),
                    )
            return bank

        def empty_bank(copy, g, b, bank):
            pair, member = divmod(g, 2)
            copy(
                out=d_grouped[pair][:, BANK_EXPERTS * b : BANK_EXPERTS * (b + 1), member, :, :],
                in_=bank[:].rearrange("p t (e c) -> p e c t", e=BANK_EXPERTS),
            )

        def quantise_dispatched(pair, e0, e1):
            nc.vector.quantize_mx(
                out=d_codes[pair][:, P * e0 : P * e1].bitcast(FP8X4),
                scales=d_scales[pair][:, P * e0 : P * e1],
                in_=d_grouped[pair][:, e0:e1, :, :, :].rearrange("p e g c t -> p (e g c t)"),
            )

        def project(pair, e, together):
            cols = slice(P * e, P * (e + 1))
            acc = psum_h.tile([P, H], F32, name="acc")
            nc.tensor.matmul_mx(
                out=acc[:],
                lhsT=d_codes[pair][:, cols].bitcast(FP8X4),
                lhsT_scale=d_scales[pair][:, cols],
                rhs=wi_codes[:, e, :].bitcast(FP8X4),
                rhs_scale=wi_planes[4 * (e % HALF) : P, e // HALF, :],
                start=True,
                stop=True,
            )
            first, place = e - e % BANK_EXPERTS, e % BANK_EXPERTS
            if place == 0:
                res[pair] = results.tile([P, BANK_EXPERTS, H], F32, name="res")
            nc.scalar.activation(out=res[pair][:, place, :], in_=acc[:], func=RELU)
            groups = slice(2 * pair, 2 * pair + 2)
            if not together:
                nc.sync.dma_start(out=out[e, groups, :, :].rearrange("g c h -> (g c) h"), in_=res[pair][:, place, :])
            elif place == BANK_EXPERTS - 1:
                nc.sync.dma_start(
                    out=out[first : e + 1, groups, :, :].rearrange("e g c h -> (g c) e h"), in_=res[pair][:]
                )

        nc.vector.memset(wi_planes[:].bitcast(I32), 0)
        for g in range(LOOKAHEAD):
            load_group(g)
            if g >= LOOKAHEAD - E // HALF:
                load_weights(g - (LOOKAHEAD - E // HALF))
        scalar_regroup(0)

        for step in range(LAST):
            if step + LOOKAHEAD < G:
                load_group(step + LOOKAHEAD)
            if step >= 1:
                for b in range(BANKS):
                    empty_bank(nc.scalar.copy, step - 1, b, dispatch_bank(step - 1, b))
            prepare(step)
            scalar_regroup(step + 1)
            if step >= 2:
                pair, half = divmod(step - 2, 2)
                for e in range(HALF * half, HALF * (half + 1)):
                    project(pair, e, True)

        prepare_x(LAST)
        for b in range(BANKS):
            empty_bank(nc.scalar.copy, LAST - 1, b, dispatch_bank(LAST - 1, b))
        banks = {}
        for b in range(BANKS + BANK_LAG):
            if b < BANKS:
                project(PAIRS - 2, HALF + b, False)
                prepare_mask_bank(LAST, b)
                banks[b] = dispatch_bank(LAST, b)
            if b >= BANK_LAG:
                d = b - BANK_LAG
                empty_bank(nc.vector.tensor_copy, LAST, d, banks[d])
                quantise_dispatched(PAIRS - 1, BANK_EXPERTS * d, BANK_EXPERTS * (d + 1))
                for e in range(BANK_EXPERTS * d, BANK_EXPERTS * (d + 1)):
                    project(PAIRS - 1, e, False)
